import numpy as np
import ml_dtypes

BF16 = ml_dtypes.bfloat16


def bf(x):
    return np.asarray(x, np.float32).astype(BF16)


def f32(x):
    return np.asarray(x, np.float32)


def f64(x):
    return np.asarray(x).astype(np.float64)


def striped(idx):
    return np.tile(idx.reshape(-1, 16).T, (8, 1))


R, S, N = 128, 4096, 512


def setup_inputs():
    return {"base": f32(np.random.standard_normal((R, S))), "moved": f32(np.random.standard_normal((R, N))), "feature_mask": f32(np.random.standard_normal((1, N))), "offs": striped(np.random.permutation(S)[:N])}


def reference(base, moved, feature_mask, offs):
    idx = offs[:16].T.reshape(-1)
    res = f64(base).copy()
    res[:, idx] = f64(moved) * (np.tanh(f64(feature_mask)) + 1.0)
    return res

@@ -1,0 +1,32 @@
+import concourse.mybir as mybir
+
+F32 = mybir.dt.float32
+U16 = mybir.dt.uint16
+
+ROWS = 128
+COLUMNS = 4096
+MOVED = 512
+
+
+def tile_shift_gcn_kernel(tc, base, moved, feature_mask, offs, out):
+    nc = tc.nc
+    with tc.tile_pool(name="held", bufs=1) as held:
+        offsets = held.tile([ROWS, MOVED // 16], U16, name="offsets")
+        nc.sync.dma_start(offsets[:], offs)
+
+        mask_rows = held.tile([ROWS, MOVED], F32, name="mask_rows")
+        nc.scalar.dma_start(mask_rows[:], feature_mask.broadcast_to([ROWS, MOVED]))
+        values = held.tile([ROWS, MOVED], F32, name="values")
+        nc.scalar.dma_start(values[:], moved)
+
+        window = held.tile([ROWS, COLUMNS], F32, name="window")
+        nc.sync.dma_start(window[:], base)
+
+        factor = held.tile([ROWS, MOVED], F32, name="factor")
+        nc.scalar.activation(factor[:], mask_rows[:], mybir.ActivationFunctionType.Tanh)
+        nc.vector.tensor_scalar_add(factor[:], factor[:], 1.0)
+
+        nc.vector.tensor_tensor(
+            window[:].indirect(offsets[:]), values[:], factor[:], mybir.AluOpType.mult
+        )
+        nc.sync.dma_start(out, window[:])

@@ -6,6 +6,7 @@ U16 = mybir.dt.uint16
 ROWS = 128
 COLUMNS = 4096
 MOVED = 512
+HALF = COLUMNS // 2
 
 
 def tile_shift_gcn_kernel(tc, base, moved, feature_mask, offs, out):
@@ -20,7 +21,8 @@ def tile_shift_gcn_kernel(tc, base, moved, feature_mask, offs, out):
         nc.scalar.dma_start(values[:], moved)
 
         window = held.tile([ROWS, COLUMNS], F32, name="window")
-        nc.sync.dma_start(window[:], base)
+        nc.sync.dma_start(window[:, :HALF], base[:, :HALF])
+        nc.scalar.dma_start(window[:, HALF:], base[:, HALF:])
 
         factor = held.tile([ROWS, MOVED], F32, name="factor")
         nc.scalar.activation(factor[:], mask_rows[:], mybir.ActivationFunctionType.Tanh)
@@ -29,4 +31,5 @@ def tile_shift_gcn_kernel(tc, base, moved, feature_mask, offs, out):
         nc.vector.tensor_tensor(
             window[:].indirect(offsets[:]), values[:], factor[:], mybir.AluOpType.mult
         )
-        nc.sync.dma_start(out, window[:])
+        nc.sync.dma_start(out[:, :HALF], window[:, :HALF])
+        nc.scalar.dma_start(out[:, HALF:], window[:, HALF:])

@@ -6,23 +6,29 @@ U16 = mybir.dt.uint16
 ROWS = 128
 COLUMNS = 4096
 MOVED = 512
-HALF = COLUMNS // 2
+
+FLOPS = ROWS * MOVED
 
 
 def tile_shift_gcn_kernel(tc, base, moved, feature_mask, offs, out):
     nc = tc.nc
-    with tc.tile_pool(name="held", bufs=1) as held:
+    with (
+        tc.tile_pool(name="held", bufs=1) as held,
+        tc.psum_pool(name="psum", bufs=1) as psum,
+    ):
         offsets = held.tile([ROWS, MOVED // 16], U16, name="offsets")
         nc.sync.dma_start(offsets[:], offs)
-
-        mask_rows = held.tile([ROWS, MOVED], F32, name="mask_rows")
-        nc.scalar.dma_start(mask_rows[:], feature_mask.broadcast_to([ROWS, MOVED]))
+        mask_row = held.tile([1, MOVED], F32, name="mask_row")
+        nc.scalar.dma_start(mask_row[:], feature_mask)
         values = held.tile([ROWS, MOVED], F32, name="values")
         nc.scalar.dma_start(values[:], moved)
-
         window = held.tile([ROWS, COLUMNS], F32, name="window")
-        nc.sync.dma_start(window[:, :HALF], base[:, :HALF])
-        nc.scalar.dma_start(window[:, HALF:], base[:, HALF:])
+        nc.sync.dma_start(window[:], base)
+
+        ones = held.tile([1, ROWS], F32, name="ones")
+        nc.vector.memset(ones[:], 1.0)
+        mask_rows = psum.tile([ROWS, MOVED], F32, name="mask_rows")
+        nc.tensor.matmul(mask_rows[:], ones[:], mask_row[:], start=True, stop=True)
 
         factor = held.tile([ROWS, MOVED], F32, name="factor")
         nc.scalar.activation(factor[:], mask_rows[:], mybir.ActivationFunctionType.Tanh)
@@ -31,5 +37,4 @@ def tile_shift_gcn_kernel(tc, base, moved, feature_mask, offs, out):
         nc.vector.tensor_tensor(
             window[:].indirect(offsets[:]), values[:], factor[:], mybir.AluOpType.mult
         )
-        nc.sync.dma_start(out[:, :HALF], window[:, :HALF])
-        nc.scalar.dma_start(out[:, HALF:], window[:, HALF:])
+        nc.sync.dma_start(out, window[:])

@@ -6,6 +6,7 @@ U16 = mybir.dt.uint16
 ROWS = 128
 COLUMNS = 4096
 MOVED = 512
+PIECE = MOVED // 4
 
 FLOPS = ROWS * MOVED
 
@@ -14,7 +15,7 @@ def tile_shift_gcn_kernel(tc, base, moved, feature_mask, offs, out):
     nc = tc.nc
     with (
         tc.tile_pool(name="held", bufs=1) as held,
-        tc.psum_pool(name="psum", bufs=1) as psum,
+        tc.psum_pool(name="psum", bufs=MOVED // PIECE) as psum,
     ):
         offsets = held.tile([ROWS, MOVED // 16], U16, name="offsets")
         nc.sync.dma_start(offsets[:], offs)
@@ -27,12 +28,15 @@ def tile_shift_gcn_kernel(tc, base, moved, feature_mask, offs, out):
 
         ones = held.tile([1, ROWS], F32, name="ones")
         nc.vector.memset(ones[:], 1.0)
-        mask_rows = psum.tile([ROWS, MOVED], F32, name="mask_rows")
-        nc.tensor.matmul(mask_rows[:], ones[:], mask_row[:], start=True, stop=True)
-
         factor = held.tile([ROWS, MOVED], F32, name="factor")
-        nc.scalar.activation(factor[:], mask_rows[:], mybir.ActivationFunctionType.Tanh)
-        nc.vector.tensor_scalar_add(factor[:], factor[:], 1.0)
+        for first in range(0, MOVED, PIECE):
+            piece = slice(first, first + PIECE)
+            mask_rows = psum.tile([ROWS, PIECE], F32, name="mask_rows")
+            nc.tensor.matmul(mask_rows[:], ones[:], mask_row[:, piece], start=True, stop=True)
+            nc.scalar.activation(
+                factor[:, piece], mask_rows[:], mybir.ActivationFunctionType.Tanh
+            )
+            nc.vector.tensor_scalar_add(factor[:, piece], factor[:, piece], 1.0)
 
         nc.vector.tensor_tensor(
             window[:].indirect(offsets[:]), values[:], factor[:], mybir.AluOpType.mult

@@ -6,7 +6,7 @@ U16 = mybir.dt.uint16
 ROWS = 128
 COLUMNS = 4096
 MOVED = 512
-PIECE = MOVED // 4
+HALF = COLUMNS // 2
 
 FLOPS = ROWS * MOVED
 
@@ -15,7 +15,7 @@ def tile_shift_gcn_kernel(tc, base, moved, feature_mask, offs, out):
     nc = tc.nc
     with (
         tc.tile_pool(name="held", bufs=1) as held,
-        tc.psum_pool(name="psum", bufs=MOVED // PIECE) as psum,
+        tc.psum_pool(name="psum", bufs=1) as psum,
     ):
         offsets = held.tile([ROWS, MOVED // 16], U16, name="offsets")
         nc.sync.dma_start(offsets[:], offs)
@@ -24,19 +24,17 @@ def tile_shift_gcn_kernel(tc, base, moved, feature_mask, offs, out):
         values = held.tile([ROWS, MOVED], F32, name="values")
         nc.scalar.dma_start(values[:], moved)
         window = held.tile([ROWS, COLUMNS], F32, name="window")
-        nc.sync.dma_start(window[:], base)
+        nc.sync.dma_start(window[:, :HALF], base[:, :HALF])
+        nc.scalar.dma_start(window[:, HALF:], base[:, HALF:])
 
         ones = held.tile([1, ROWS], F32, name="ones")
         nc.vector.memset(ones[:], 1.0)
+        mask_rows = psum.tile([ROWS, MOVED], F32, name="mask_rows")
+        nc.tensor.matmul(mask_rows[:], ones[:], mask_row[:], start=True, stop=True)
+
         factor = held.tile([ROWS, MOVED], F32, name="factor")
-        for first in range(0, MOVED, PIECE):
-            piece = slice(first, first + PIECE)
-            mask_rows = psum.tile([ROWS, PIECE], F32, name="mask_rows")
-            nc.tensor.matmul(mask_rows[:], ones[:], mask_row[:, piece], start=True, stop=True)
-            nc.scalar.activation(
-                factor[:, piece], mask_rows[:], mybir.ActivationFunctionType.Tanh
-            )
-            nc.vector.tensor_scalar_add(factor[:, piece], factor[:, piece], 1.0)
+        nc.scalar.activation(factor[:], mask_rows[:], mybir.ActivationFunctionType.Tanh)
+        nc.vector.tensor_scalar_add(factor[:], factor[:], 1.0)
 
         nc.vector.tensor_tensor(
             window[:].indirect(offsets[:]), values[:], factor[:], mybir.AluOpType.mult

@@ -6,7 +6,6 @@ U16 = mybir.dt.uint16
 ROWS = 128
 COLUMNS = 4096
 MOVED = 512
-HALF = COLUMNS // 2
 
 FLOPS = ROWS * MOVED
 
@@ -17,15 +16,14 @@ def tile_shift_gcn_kernel(tc, base, moved, feature_mask, offs, out):
         tc.tile_pool(name="held", bufs=1) as held,
         tc.psum_pool(name="psum", bufs=1) as psum,
     ):
+        window = held.tile([ROWS, COLUMNS], F32, name="window")
+        nc.scalar.dma_start(window[:], base)
+        mask_row = held.tile([1, MOVED], F32, name="mask_row")
+        nc.sync.dma_start(mask_row[:], feature_mask)
         offsets = held.tile([ROWS, MOVED // 16], U16, name="offsets")
         nc.sync.dma_start(offsets[:], offs)
-        mask_row = held.tile([1, MOVED], F32, name="mask_row")
-        nc.scalar.dma_start(mask_row[:], feature_mask)
         values = held.tile([ROWS, MOVED], F32, name="values")
-        nc.scalar.dma_start(values[:], moved)
-        window = held.tile([ROWS, COLUMNS], F32, name="window")
-        nc.sync.dma_start(window[:, :HALF], base[:, :HALF])
-        nc.scalar.dma_start(window[:, HALF:], base[:, HALF:])
+        nc.sync.dma_start(values[:], moved)
 
         ones = held.tile([1, ROWS], F32, name="ones")
         nc.vector.memset(ones[:], 1.0)

@@ -6,6 +6,7 @@ U16 = mybir.dt.uint16
 ROWS = 128
 COLUMNS = 4096
 MOVED = 512
+WINDOWS = 2
 
 FLOPS = ROWS * MOVED
 
@@ -16,8 +17,9 @@ def tile_shift_gcn_kernel(tc, base, moved, feature_mask, offs, out):
         tc.tile_pool(name="held", bufs=1) as held,
         tc.psum_pool(name="psum", bufs=1) as psum,
     ):
-        window = held.tile([ROWS, COLUMNS], F32, name="window")
-        nc.scalar.dma_start(window[:], base)
+        windows = [held.tile([ROWS, COLUMNS], F32, name="window%d" % w) for w in range(WINDOWS)]
+        for w in range(WINDOWS):
+            nc.scalar.dma_start(windows[w][w:ROWS:WINDOWS, :], base[w:ROWS:WINDOWS, :])
         mask_row = held.tile([1, MOVED], F32, name="mask_row")
         nc.sync.dma_start(mask_row[:], feature_mask)
         offsets = held.tile([ROWS, MOVED // 16], U16, name="offsets")
@@ -34,7 +36,8 @@ def tile_shift_gcn_kernel(tc, base, moved, feature_mask, offs, out):
         nc.scalar.activation(factor[:], mask_rows[:], mybir.ActivationFunctionType.Tanh)
         nc.vector.tensor_scalar_add(factor[:], factor[:], 1.0)
 
-        nc.vector.tensor_tensor(
-            window[:].indirect(offsets[:]), values[:], factor[:], mybir.AluOpType.mult
-        )
-        nc.sync.dma_start(out, window[:])
+        for w in range(WINDOWS):
+            nc.vector.tensor_tensor(
+                windows[w][:].indirect(offsets[:]), values[:], factor[:], mybir.AluOpType.mult
+            )
+            nc.sync.dma_start(out[w:ROWS:WINDOWS, :], windows[w][w:ROWS:WINDOWS, :])

@@ -6,7 +6,8 @@ U16 = mybir.dt.uint16
 ROWS = 128
 COLUMNS = 4096
 MOVED = 512
-WINDOWS = 2
+
+ROW_GROUPS = (((0, 2), (1, 4)), ((3, 4),))
 
 FLOPS = ROWS * MOVED
 
@@ -17,9 +18,10 @@ def tile_shift_gcn_kernel(tc, base, moved, feature_mask, offs, out):
         tc.tile_pool(name="held", bufs=1) as held,
         tc.psum_pool(name="psum", bufs=1) as psum,
     ):
-        windows = [held.tile([ROWS, COLUMNS], F32, name="window%d" % w) for w in range(WINDOWS)]
-        for w in range(WINDOWS):
-            nc.scalar.dma_start(windows[w][w:ROWS:WINDOWS, :], base[w:ROWS:WINDOWS, :])
+        windows = [held.tile([ROWS, COLUMNS], F32, name="window%d" % w) for w in range(2)]
+
+        for first, step in ROW_GROUPS[0]:
+            nc.scalar.dma_start(windows[0][first:ROWS:step, :], base[first:ROWS:step, :])
         mask_row = held.tile([1, MOVED], F32, name="mask_row")
         nc.sync.dma_start(mask_row[:], feature_mask)
         offsets = held.tile([ROWS, MOVED // 16], U16, name="offsets")
@@ -36,8 +38,12 @@ def tile_shift_gcn_kernel(tc, base, moved, feature_mask, offs, out):
         nc.scalar.activation(factor[:], mask_rows[:], mybir.ActivationFunctionType.Tanh)
         nc.vector.tensor_scalar_add(factor[:], factor[:], 1.0)
 
-        for w in range(WINDOWS):
+        for first, step in ROW_GROUPS[1]:
+            nc.scalar.dma_start(windows[1][first:ROWS:step, :], base[first:ROWS:step, :])
+
+        for w in range(2):
             nc.vector.tensor_tensor(
                 windows[w][:].indirect(offsets[:]), values[:], factor[:], mybir.AluOpType.mult
             )
-            nc.sync.dma_start(out[w:ROWS:WINDOWS, :], windows[w][w:ROWS:WINDOWS, :])
+            for first, step in ROW_GROUPS[w]:
+                nc.sync.dma_start(out[first:ROWS:step, :], windows[w][first:ROWS:step, :])

@@ -6,6 +6,7 @@ U16 = mybir.dt.uint16
 ROWS = 128
 COLUMNS = 4096
 MOVED = 512
+PIECE = 128
 
 ROW_GROUPS = (((0, 2), (1, 4)), ((3, 4),))
 
@@ -16,7 +17,7 @@ def tile_shift_gcn_kernel(tc, base, moved, feature_mask, offs, out):
     nc = tc.nc
     with (
         tc.tile_pool(name="held", bufs=1) as held,
-        tc.psum_pool(name="psum", bufs=1) as psum,
+        tc.psum_pool(name="psum", bufs=MOVED // PIECE) as psum,
     ):
         windows = [held.tile([ROWS, COLUMNS], F32, name="window%d" % w) for w in range(2)]
 
@@ -31,12 +32,16 @@ def tile_shift_gcn_kernel(tc, base, moved, feature_mask, offs, out):
 
         ones = held.tile([1, ROWS], F32, name="ones")
         nc.vector.memset(ones[:], 1.0)
-        mask_rows = psum.tile([ROWS, MOVED], F32, name="mask_rows")
-        nc.tensor.matmul(mask_rows[:], ones[:], mask_row[:], start=True, stop=True)
 
         factor = held.tile([ROWS, MOVED], F32, name="factor")
-        nc.scalar.activation(factor[:], mask_rows[:], mybir.ActivationFunctionType.Tanh)
-        nc.vector.tensor_scalar_add(factor[:], factor[:], 1.0)
+        for start in range(0, MOVED, PIECE):
+            piece = slice(start, start + PIECE)
+            mask_rows = psum.tile([ROWS, PIECE], F32, name="mask_rows")
+            nc.tensor.matmul(mask_rows[:], ones[:], mask_row[:, piece], start=True, stop=True)
+            nc.scalar.activation(
+                factor[:, piece], mask_rows[:], mybir.ActivationFunctionType.Tanh
+            )
+            nc.vector.tensor_scalar_add(factor[:, piece], factor[:, piece], 1.0)
 
         for first, step in ROW_GROUPS[1]:
             nc.scalar.dma_start(windows[1][first:ROWS:step, :], base[first:ROWS:step, :])

@@ -1,4 +1,5 @@
 import concourse.mybir as mybir
+from concourse.masks import make_identity
 
 F32 = mybir.dt.float32
 U16 = mybir.dt.uint16
@@ -6,9 +7,8 @@ U16 = mybir.dt.uint16
 ROWS = 128
 COLUMNS = 4096
 MOVED = 512
-PIECE = 128
-
-ROW_GROUPS = (((0, 2), (1, 4)), ((3, 4),))
+WINDOWS = 2
+FOLD = MOVED // ROWS
 
 FLOPS = ROWS * MOVED
 
@@ -17,38 +17,43 @@ def tile_shift_gcn_kernel(tc, base, moved, feature_mask, offs, out):
     nc = tc.nc
     with (
         tc.tile_pool(name="held", bufs=1) as held,
-        tc.psum_pool(name="psum", bufs=MOVED // PIECE) as psum,
+        tc.psum_pool(name="psum", bufs=1) as psum,
     ):
-        windows = [held.tile([ROWS, COLUMNS], F32, name="window%d" % w) for w in range(2)]
+        windows = [held.tile([ROWS, COLUMNS], F32, name="window%d" % w) for w in range(WINDOWS)]
 
-        for first, step in ROW_GROUPS[0]:
-            nc.scalar.dma_start(windows[0][first:ROWS:step, :], base[first:ROWS:step, :])
-        mask_row = held.tile([1, MOVED], F32, name="mask_row")
-        nc.sync.dma_start(mask_row[:], feature_mask)
+        nc.scalar.dma_start(windows[0][0:ROWS:WINDOWS, :], base[0:ROWS:WINDOWS, :])
+        mask_folded = held.tile([ROWS, FOLD], F32, name="mask_folded")
+        nc.sync.dma_start(mask_folded[:], feature_mask.rearrange("o (p f) -> p (o f)", f=FOLD))
         offsets = held.tile([ROWS, MOVED // 16], U16, name="offsets")
         nc.sync.dma_start(offsets[:], offs)
         values = held.tile([ROWS, MOVED], F32, name="values")
         nc.sync.dma_start(values[:], moved)
 
-        ones = held.tile([1, ROWS], F32, name="ones")
-        nc.vector.memset(ones[:], 1.0)
+        identity = held.tile([ROWS, ROWS], F32, name="identity")
+        make_identity(nc, identity[:])
+
+        tanh_folded = held.tile([ROWS, FOLD], F32, name="tanh_folded")
+        nc.scalar.activation(tanh_folded[:], mask_folded[:], mybir.ActivationFunctionType.Tanh)
+
+        nc.scalar.dma_start(windows[1][1:ROWS:WINDOWS, :], base[1:ROWS:WINDOWS, :])
+
+        tanh_rows = psum.tile([ROWS, FOLD, ROWS], F32, name="tanh_rows")
+        for f in range(FOLD):
+            nc.tensor.transpose(
+                tanh_rows[:, f, :],
+                tanh_folded[:, f : f + 1].to_broadcast([ROWS, ROWS]),
+                identity[:],
+            )
 
         factor = held.tile([ROWS, MOVED], F32, name="factor")
-        for start in range(0, MOVED, PIECE):
-            piece = slice(start, start + PIECE)
-            mask_rows = psum.tile([ROWS, PIECE], F32, name="mask_rows")
-            nc.tensor.matmul(mask_rows[:], ones[:], mask_row[:, piece], start=True, stop=True)
-            nc.scalar.activation(
-                factor[:, piece], mask_rows[:], mybir.ActivationFunctionType.Tanh
-            )
-            nc.vector.tensor_scalar_add(factor[:, piece], factor[:, piece], 1.0)
+        nc.vector.tensor_scalar_add(
+            factor[:].rearrange("r (p f) -> r p f", f=FOLD),
+            tanh_rows[:].rearrange("r f p -> r p f"),
+            1.0,
+        )
 
-        for first, step in ROW_GROUPS[1]:
-            nc.scalar.dma_start(windows[1][first:ROWS:step, :], base[first:ROWS:step, :])
-
-        for w in range(2):
+        for w in range(WINDOWS):
             nc.vector.tensor_tensor(
                 windows[w][:].indirect(offsets[:]), values[:], factor[:], mybir.AluOpType.mult
             )
-            for first, step in ROW_GROUPS[w]:
-                nc.sync.dma_start(out[first:ROWS:step, :], windows[w][first:ROWS:step, :])
+            nc.sync.dma_start(out[w:ROWS:WINDOWS, :], windows[w][w:ROWS:WINDOWS, :])

@@ -26,8 +26,10 @@ def tile_shift_gcn_kernel(tc, base, moved, feature_mask, offs, out):
         nc.sync.dma_start(mask_folded[:], feature_mask.rearrange("o (p f) -> p (o f)", f=FOLD))
         offsets = held.tile([ROWS, MOVED // 16], U16, name="offsets")
         nc.sync.dma_start(offsets[:], offs)
-        values = held.tile([ROWS, MOVED], F32, name="values")
-        nc.sync.dma_start(values[:], moved)
+        values = [held.tile([ROWS, MOVED], F32, name="values%d" % w) for w in range(WINDOWS)]
+        for w in range(WINDOWS):
+            nc.vector.memset(values[w][:], 0.0)
+        nc.sync.dma_start(values[0][0:ROWS:WINDOWS, :], moved[0:ROWS:WINDOWS, :])
 
         identity = held.tile([ROWS, ROWS], F32, name="identity")
         make_identity(nc, identity[:])
@@ -36,6 +38,7 @@ def tile_shift_gcn_kernel(tc, base, moved, feature_mask, offs, out):
         nc.scalar.activation(tanh_folded[:], mask_folded[:], mybir.ActivationFunctionType.Tanh)
 
         nc.scalar.dma_start(windows[1][1:ROWS:WINDOWS, :], base[1:ROWS:WINDOWS, :])
+        nc.scalar.dma_start(values[1][1:ROWS:WINDOWS, :], moved[1:ROWS:WINDOWS, :])
 
         tanh_rows = psum.tile([ROWS, FOLD, ROWS], F32, name="tanh_rows")
         for f in range(FOLD):
@@ -54,6 +57,6 @@ def tile_shift_gcn_kernel(tc, base, moved, feature_mask, offs, out):
 
         for w in range(WINDOWS):
             nc.vector.tensor_tensor(
-                windows[w][:].indirect(offsets[:]), values[:], factor[:], mybir.AluOpType.mult
+                windows[w][:].indirect(offsets[:]), values[w][:], factor[:], mybir.AluOpType.mult
             )
             nc.sync.dma_start(out[w:ROWS:WINDOWS, :], windows[w][w:ROWS:WINDOWS, :])

@@ -8,7 +8,8 @@ ROWS = 128
 COLUMNS = 4096
 MOVED = 512
 WINDOWS = 2
-FOLD = MOVED // ROWS
+FOLDED_ROWS = 64
+FOLD = MOVED // FOLDED_ROWS
 
 FLOPS = ROWS * MOVED
 
@@ -22,7 +23,7 @@ def tile_shift_gcn_kernel(tc, base, moved, feature_mask, offs, out):
         windows = [held.tile([ROWS, COLUMNS], F32, name="window%d" % w) for w in range(WINDOWS)]
 
         nc.scalar.dma_start(windows[0][0:ROWS:WINDOWS, :], base[0:ROWS:WINDOWS, :])
-        mask_folded = held.tile([ROWS, FOLD], F32, name="mask_folded")
+        mask_folded = held.tile([FOLDED_ROWS, FOLD], F32, name="mask_folded")
         nc.sync.dma_start(mask_folded[:], feature_mask.rearrange("o (p f) -> p (o f)", f=FOLD))
         offsets = held.tile([ROWS, MOVED // 16], U16, name="offsets")
         nc.sync.dma_start(offsets[:], offs)
@@ -31,20 +32,20 @@ def tile_shift_gcn_kernel(tc, base, moved, feature_mask, offs, out):
             nc.vector.memset(values[w][:], 0.0)
         nc.sync.dma_start(values[0][0:ROWS:WINDOWS, :], moved[0:ROWS:WINDOWS, :])
 
-        identity = held.tile([ROWS, ROWS], F32, name="identity")
+        identity = held.tile([FOLDED_ROWS, FOLDED_ROWS], F32, name="identity")
         make_identity(nc, identity[:])
 
-        tanh_folded = held.tile([ROWS, FOLD], F32, name="tanh_folded")
+        tanh_folded = held.tile([FOLDED_ROWS, FOLD], F32, name="tanh_folded")
         nc.scalar.activation(tanh_folded[:], mask_folded[:], mybir.ActivationFunctionType.Tanh)
 
         nc.scalar.dma_start(windows[1][1:ROWS:WINDOWS, :], base[1:ROWS:WINDOWS, :])
         nc.scalar.dma_start(values[1][1:ROWS:WINDOWS, :], moved[1:ROWS:WINDOWS, :])
 
-        tanh_rows = psum.tile([ROWS, FOLD, ROWS], F32, name="tanh_rows")
+        tanh_rows = psum.tile([ROWS, FOLD, FOLDED_ROWS], F32, name="tanh_rows")
         for f in range(FOLD):
             nc.tensor.transpose(
                 tanh_rows[:, f, :],
-                tanh_folded[:, f : f + 1].to_broadcast([ROWS, ROWS]),
+                tanh_folded[:, f : f + 1].to_broadcast([FOLDED_ROWS, ROWS]),
                 identity[:],
             )
 

@@ -10,6 +10,8 @@ MOVED = 512
 WINDOWS = 2
 FOLDED_ROWS = 64
 FOLD = MOVED // FOLDED_ROWS
+HALVES = 2
+HALF_FOLD = FOLD // HALVES
 
 FLOPS = ROWS * MOVED
 
@@ -41,23 +43,27 @@ def tile_shift_gcn_kernel(tc, base, moved, feature_mask, offs, out):
         nc.scalar.dma_start(windows[1][1:ROWS:WINDOWS, :], base[1:ROWS:WINDOWS, :])
         nc.scalar.dma_start(values[1][1:ROWS:WINDOWS, :], moved[1:ROWS:WINDOWS, :])
 
-        tanh_rows = psum.tile([ROWS, FOLD, FOLDED_ROWS], F32, name="tanh_rows")
-        for f in range(FOLD):
-            nc.tensor.transpose(
-                tanh_rows[:, f, :],
-                tanh_folded[:, f : f + 1].to_broadcast([FOLDED_ROWS, ROWS]),
-                identity[:],
+        factor = held.tile([ROWS, FOLDED_ROWS, FOLD], F32, name="factor")
+        for h in range(HALVES):
+            tanh_rows = psum.tile([ROWS, HALF_FOLD, FOLDED_ROWS], F32, name="tanh_rows%d" % h)
+            for f in range(HALF_FOLD):
+                column = h * HALF_FOLD + f
+                nc.tensor.transpose(
+                    tanh_rows[:, f, :],
+                    tanh_folded[:, column : column + 1].to_broadcast([FOLDED_ROWS, ROWS]),
+                    identity[:],
+                )
+            nc.vector.tensor_scalar_add(
+                factor[:, :, h * HALF_FOLD : (h + 1) * HALF_FOLD],
+                tanh_rows[:].rearrange("r f p -> r p f"),
+                1.0,
             )
-
-        factor = held.tile([ROWS, MOVED], F32, name="factor")
-        nc.vector.tensor_scalar_add(
-            factor[:].rearrange("r (p f) -> r p f", f=FOLD),
-            tanh_rows[:].rearrange("r f p -> r p f"),
-            1.0,
-        )
 
         for w in range(WINDOWS):
             nc.vector.tensor_tensor(
-                windows[w][:].indirect(offsets[:]), values[w][:], factor[:], mybir.AluOpType.mult
+                windows[w][:].indirect(offsets[:]),
+                values[w][:],
+                factor[:].rearrange("r p f -> r (p f)"),
+                mybir.AluOpType.mult,
             )
             nc.sync.dma_start(out[w:ROWS:WINDOWS, :], windows[w][w:ROWS:WINDOWS, :])

@@ -27,12 +27,12 @@ def tile_shift_gcn_kernel(tc, base, moved, feature_mask, offs, out):
         nc.scalar.dma_start(windows[0][0:ROWS:WINDOWS, :], base[0:ROWS:WINDOWS, :])
         mask_folded = held.tile([FOLDED_ROWS, FOLD], F32, name="mask_folded")
         nc.sync.dma_start(mask_folded[:], feature_mask.rearrange("o (p f) -> p (o f)", f=FOLD))
-        offsets = held.tile([ROWS, MOVED // 16], U16, name="offsets")
-        nc.sync.dma_start(offsets[:], offs)
         values = [held.tile([ROWS, MOVED], F32, name="values%d" % w) for w in range(WINDOWS)]
         for w in range(WINDOWS):
             nc.vector.memset(values[w][:], 0.0)
         nc.sync.dma_start(values[0][0:ROWS:WINDOWS, :], moved[0:ROWS:WINDOWS, :])
+        offsets = held.tile([ROWS, MOVED // 16], U16, name="offsets")
+        nc.sync.dma_start(offsets[:], offs)
 
         identity = held.tile([FOLDED_ROWS, FOLDED_ROWS], F32, name="identity")
         make_identity(nc, identity[:])

@@ -24,24 +24,23 @@ def tile_shift_gcn_kernel(tc, base, moved, feature_mask, offs, out):
     ):
         windows = [held.tile([ROWS, COLUMNS], F32, name="window%d" % w) for w in range(WINDOWS)]
 
-        nc.scalar.dma_start(windows[0][0:ROWS:WINDOWS, :], base[0:ROWS:WINDOWS, :])
         mask_folded = held.tile([FOLDED_ROWS, FOLD], F32, name="mask_folded")
         nc.sync.dma_start(mask_folded[:], feature_mask.rearrange("o (p f) -> p (o f)", f=FOLD))
+        nc.sync.dma_start(windows[0][0:ROWS:WINDOWS, :], base[0:ROWS:WINDOWS, :])
         values = [held.tile([ROWS, MOVED], F32, name="values%d" % w) for w in range(WINDOWS)]
         for w in range(WINDOWS):
             nc.vector.memset(values[w][:], 0.0)
         nc.sync.dma_start(values[0][0:ROWS:WINDOWS, :], moved[0:ROWS:WINDOWS, :])
         offsets = held.tile([ROWS, MOVED // 16], U16, name="offsets")
         nc.sync.dma_start(offsets[:], offs)
+        nc.sync.dma_start(windows[1][1:ROWS:WINDOWS, :], base[1:ROWS:WINDOWS, :])
+        nc.sync.dma_start(values[1][1:ROWS:WINDOWS, :], moved[1:ROWS:WINDOWS, :])
 
         identity = held.tile([FOLDED_ROWS, FOLDED_ROWS], F32, name="identity")
         make_identity(nc, identity[:])
 
         tanh_folded = held.tile([FOLDED_ROWS, FOLD], F32, name="tanh_folded")
         nc.scalar.activation(tanh_folded[:], mask_folded[:], mybir.ActivationFunctionType.Tanh)
-
-        nc.scalar.dma_start(windows[1][1:ROWS:WINDOWS, :], base[1:ROWS:WINDOWS, :])
-        nc.scalar.dma_start(values[1][1:ROWS:WINDOWS, :], moved[1:ROWS:WINDOWS, :])
 
         factor = held.tile([ROWS, FOLDED_ROWS, FOLD], F32, name="factor")
         for h in range(HALVES):

@@ -8,10 +8,7 @@ ROWS = 128
 COLUMNS = 4096
 MOVED = 512
 WINDOWS = 2
-FOLDED_ROWS = 64
-FOLD = MOVED // FOLDED_ROWS
-HALVES = 2
-HALF_FOLD = FOLD // HALVES
+FOLD = MOVED // ROWS
 
 FLOPS = ROWS * MOVED
 
@@ -24,7 +21,7 @@ def tile_shift_gcn_kernel(tc, base, moved, feature_mask, offs, out):
     ):
         windows = [held.tile([ROWS, COLUMNS], F32, name="window%d" % w) for w in range(WINDOWS)]
 
-        mask_folded = held.tile([FOLDED_ROWS, FOLD], F32, name="mask_folded")
+        mask_folded = held.tile([ROWS, FOLD], F32, name="mask_folded")
         nc.sync.dma_start(mask_folded[:], feature_mask.rearrange("o (p f) -> p (o f)", f=FOLD))
         nc.sync.dma_start(windows[0][0:ROWS:WINDOWS, :], base[0:ROWS:WINDOWS, :])
         values = [held.tile([ROWS, MOVED], F32, name="values%d" % w) for w in range(WINDOWS)]
@@ -36,33 +33,29 @@ def tile_shift_gcn_kernel(tc, base, moved, feature_mask, offs, out):
         nc.sync.dma_start(windows[1][1:ROWS:WINDOWS, :], base[1:ROWS:WINDOWS, :])
         nc.sync.dma_start(values[1][1:ROWS:WINDOWS, :], moved[1:ROWS:WINDOWS, :])
 
-        identity = held.tile([FOLDED_ROWS, FOLDED_ROWS], F32, name="identity")
+        identity = held.tile([ROWS, ROWS], F32, name="identity")
         make_identity(nc, identity[:])
 
-        tanh_folded = held.tile([FOLDED_ROWS, FOLD], F32, name="tanh_folded")
+        tanh_folded = held.tile([ROWS, FOLD], F32, name="tanh_folded")
         nc.scalar.activation(tanh_folded[:], mask_folded[:], mybir.ActivationFunctionType.Tanh)
 
-        factor = held.tile([ROWS, FOLDED_ROWS, FOLD], F32, name="factor")
-        for h in range(HALVES):
-            tanh_rows = psum.tile([ROWS, HALF_FOLD, FOLDED_ROWS], F32, name="tanh_rows%d" % h)
-            for f in range(HALF_FOLD):
-                column = h * HALF_FOLD + f
-                nc.tensor.transpose(
-                    tanh_rows[:, f, :],
-                    tanh_folded[:, column : column + 1].to_broadcast([FOLDED_ROWS, ROWS]),
-                    identity[:],
-                )
-            nc.vector.tensor_scalar_add(
-                factor[:, :, h * HALF_FOLD : (h + 1) * HALF_FOLD],
-                tanh_rows[:].rearrange("r f p -> r p f"),
-                1.0,
+        tanh_rows = psum.tile([ROWS, FOLD, ROWS], F32, name="tanh_rows")
+        for f in range(FOLD):
+            nc.tensor.transpose(
+                tanh_rows[:, f, :],
+                tanh_folded[:, f : f + 1].to_broadcast([ROWS, ROWS]),
+                identity[:],
             )
+
+        factor = held.tile([ROWS, MOVED], F32, name="factor")
+        nc.vector.tensor_scalar_add(
+            factor[:].rearrange("r (p f) -> r p f", f=FOLD),
+            tanh_rows[:].rearrange("r f p -> r p f"),
+            1.0,
+        )
 
         for w in range(WINDOWS):
             nc.vector.tensor_tensor(
-                windows[w][:].indirect(offsets[:]),
-                values[w][:],
-                factor[:].rearrange("r p f -> r (p f)"),
-                mybir.AluOpType.mult,
+                windows[w][:].indirect(offsets[:]), values[w][:], factor[:], mybir.AluOpType.mult
             )
             nc.sync.dma_start(out[w:ROWS:WINDOWS, :], windows[w][w:ROWS:WINDOWS, :])

import concourse.mybir as mybir
from concourse.masks import make_identity

F32 = mybir.dt.float32
U16 = mybir.dt.uint16

ROWS = 128
COLUMNS = 4096
MOVED = 512
WINDOWS = 2
FOLD = MOVED // ROWS

FLOPS = ROWS * MOVED


def tile_shift_gcn_kernel(tc, base, moved, feature_mask, offs, out):
    nc = tc.nc
    with (
        tc.tile_pool(name="held", bufs=1) as held,
        tc.psum_pool(name="psum", bufs=1) as psum,
    ):
        windows = [held.tile([ROWS, COLUMNS], F32, name="window%d" % w) for w in range(WINDOWS)]

        mask_folded = held.tile([ROWS, FOLD], F32, name="mask_folded")
        nc.sync.dma_start(mask_folded[:], feature_mask.rearrange("o (p f) -> p (o f)", f=FOLD))
        nc.sync.dma_start(windows[0][0:ROWS:WINDOWS, :], base[0:ROWS:WINDOWS, :])
        values = [held.tile([ROWS, MOVED], F32, name="values%d" % w) for w in range(WINDOWS)]
        for w in range(WINDOWS):
            nc.vector.memset(values[w][:], 0.0)
        nc.sync.dma_start(values[0][0:ROWS:WINDOWS, :], moved[0:ROWS:WINDOWS, :])
        offsets = held.tile([ROWS, MOVED // 16], U16, name="offsets")
        nc.sync.dma_start(offsets[:], offs)
        nc.sync.dma_start(windows[1][1:ROWS:WINDOWS, :], base[1:ROWS:WINDOWS, :])
        nc.sync.dma_start(values[1][1:ROWS:WINDOWS, :], moved[1:ROWS:WINDOWS, :])

        identity = held.tile([ROWS, ROWS], F32, name="identity")
        make_identity(nc, identity[:])

        tanh_folded = held.tile([ROWS, FOLD], F32, name="tanh_folded")
        nc.scalar.activation(tanh_folded[:], mask_folded[:], mybir.ActivationFunctionType.Tanh)

        tanh_rows = psum.tile([ROWS, FOLD, ROWS], F32, name="tanh_rows")
        for f in range(FOLD):
            nc.tensor.transpose(
                tanh_rows[:, f, :],
                tanh_folded[:, f : f + 1].to_broadcast([ROWS, ROWS]),
                identity[:],
            )

        factor = held.tile([ROWS, MOVED], F32, name="factor")
        nc.vector.tensor_scalar_add(
            factor[:].rearrange("r (p f) -> r p f", f=FOLD),
            tanh_rows[:].rearrange("r f p -> r p f"),
            1.0,
        )

        for w in range(WINDOWS):
            nc.vector.tensor_tensor(
                windows[w][:].indirect(offsets[:]), values[w][:], factor[:], mybir.AluOpType.mult
            )
            nc.sync.dma_start(out[w:ROWS:WINDOWS, :], windows[w][w:ROWS:WINDOWS, :])
